import numpy as np
import ml_dtypes


def mxq(x, axis, fmt="e4m3"):
    dtype, down = {"e4m3": (ml_dtypes.float8_e4m3fn, 7), "e5m2": (ml_dtypes.float8_e5m2, 14)}[fmt]
    v = np.moveaxis(np.asarray(x, np.float32).astype(ml_dtypes.bfloat16).astype(np.float64), axis, -1)
    blocks = v.reshape(v.shape[:-1] + (-1, 32))
    amax = np.abs(blocks).max(-1, keepdims=True)
    byte = np.maximum(np.where(amax > 0, np.frexp(amax)[1] - 1 + 127, 0) - down, 1)
    scale = np.exp2(byte - 127.0)
    codes = (blocks / scale).astype(np.float32).astype(dtype).astype(np.float64)
    return np.moveaxis((codes * scale).reshape(v.shape), -1, axis)


WIDE = False


def mx_kscale(k):
    if not WIDE:
        return np.ones(k)
    levels = np.array([10, -10, 5, -5, 0])
    if k % 512:
        return np.exp2(np.random.permutation(np.resize(levels, k // 32))).repeat(32)
    a = np.empty((k // 512, 16))
    for p in range(k // 512):
        a[p, :8] = np.random.permutation(np.resize(levels, 8))
        for g in range(8):
            far = levels[np.abs(levels - a[p, g]) >= 10]
            a[p, g + 8] = far[np.random.randint(len(far))]
    return np.exp2(a.ravel()).repeat(32)


BF16 = ml_dtypes.bfloat16


def bf(x):
    return np.asarray(x, np.float32).astype(BF16)


def f64(x):
    return np.asarray(x).astype(np.float64)


I, H, B = 2048, 2048, 128


def sigmoid(v):
    return 1.0 / (1.0 + np.exp(-v))


def setup_inputs():
    s, t = mx_kscale(I), mx_kscale(H)
    d = {"x": bf(np.random.standard_normal((I, B)) * s[:, None]), "h": bf(np.random.standard_normal((B, H)) * t[None, :])}
    for n in ("w_ii", "w_ig"):
        d[n] = bf(np.random.standard_normal((H, I)) * 0.7 / np.sqrt(I) / s[None, :])
    for n in ("w_hi", "w_hg"):
        d[n] = bf(np.random.standard_normal((H, H)) * 0.7 / np.sqrt(H) / t[None, :])
    for n in ("b_ii", "b_hi", "b_ig", "b_hg"):
        d[n] = bf(np.random.standard_normal((H, 1)) * 0.3)
    return d


def core(x, h, w_ii, w_ig, w_hi, w_hg, b_ii, b_hi, b_ig, b_hg):
    xq = mxq(f64(x), 0, "e4m3")
    hq = mxq(f64(h).T, 0, "e4m3")
    i = sigmoid((mxq(f64(w_ii), 1, "e4m3") @ xq) + f64(b_ii) + (mxq(f64(w_hi), 1, "e4m3") @ hq) + f64(b_hi))
    g = np.tanh((mxq(f64(w_ig), 1, "e4m3") @ xq) + f64(b_ig) + (mxq(f64(w_hg), 1, "e4m3") @ hq) + f64(b_hg))
    return i * g


def e4m3fn_bytes(y):
    return np.clip(np.asarray(y, np.float64), -448.0, 448.0).astype(np.float32).astype(ml_dtypes.float8_e4m3fn).view(np.uint8)


def reference(x, h, w_ii, w_ig, w_hi, w_hg, b_ii, b_hi, b_ig, b_hg):
    out = core(x, h, w_ii, w_ig, w_hi, w_hg, b_ii, b_hi, b_ig, b_hg)
    s = np.max(np.abs(out)) / 448.0
    return out, e4m3fn_bytes(out / s)

@@ -1,0 +1,271 @@
+from contextlib import ExitStack
+
+import concourse.mybir as mybir
+from concourse.masks import make_identity
+
+FLOPS = 4 * 2 * 2048 * 2048 * 128
+
+F32 = mybir.dt.float32
+BF16 = mybir.dt.bfloat16
+U32 = mybir.dt.uint32
+U8 = mybir.dt.uint8
+FP8X4 = mybir.dt.float8_e4m3fn_x4
+FP8 = mybir.dt.float8_e4m3fn
+ALU = mybir.AluOpType
+ACT = mybir.ActivationFunctionType
+AX = mybir.AxisListType
+
+P = 128
+K = 2048
+B = 128
+J = 16
+WORDS = K // 2
+PASSES = 4
+STEPS = 32
+RAW_BUFS = 10
+LOAD_AHEAD = RAW_BUFS // 2 - 1
+V_CAST = 1408
+
+
+def perm_flags(t):
+    return (False, False)
+
+
+def evac_engines(t):
+    return "SSSV"
+
+
+def load_split(ss):
+    return 2 if ss == 0 or ss == STEPS // 2 - 1 else 1
+
+
+def tile_naivelstm_pa_kernel(tc, x, h, w_ii, w_ig, w_hi, w_hg, b_ii, b_hi, b_ig, b_hg, out_0, out_1):
+    nc = tc.nc
+    wx = [w_ii.rearrange("(p j) k -> p j k", j=J), w_ig.rearrange("(p j) k -> p j k", j=J)]
+    wh = [w_hi.rearrange("(p j) k -> p j k", j=J), w_hg.rearrange("(p j) k -> p j k", j=J)]
+    out0_v = out_0.rearrange("(p j) b -> p j b", j=J)
+    out1_v = out_1.rearrange("(p j) b -> p j b", j=J)
+
+    with ExitStack() as ctx:
+        const = ctx.enter_context(tc.tile_pool(name="const", bufs=1))
+        rawp = ctx.enter_context(tc.tile_pool(name="rawp", bufs=RAW_BUFS))
+        permp = ctx.enter_context(tc.tile_pool(name="permp", bufs=8))
+        grpp = ctx.enter_context(tc.tile_pool(name="grpp", bufs=6))
+        codep = ctx.enter_context(tc.tile_pool(name="codep", bufs=6))
+        gatep = ctx.enter_context(tc.tile_pool(name="gatep", bufs=2))
+        trp = ctx.enter_context(tc.psum_pool(name="trp", bufs=6))
+        accp = ctx.enter_context(tc.psum_pool(name="accp", bufs=1))
+
+        ident = const.tile([P, P], F32, name="ident")
+        make_identity(nc, ident[:])
+        zero = const.tile([P, 1], F32, name="zero")
+        nc.vector.memset(zero[:], 0.0)
+        warm = const.tile([P, 1], F32, name="warm")
+
+        bias_raw = []
+        for n, b_ap in enumerate((b_ii, b_hi, b_ig, b_hg)):
+            bt = const.tile([P, J], BF16, name="bias_raw%d" % n)
+            nc.scalar.dma_start(out=bt[:], in_=b_ap.rearrange("(p j) o -> p (j o)", j=J))
+            bias_raw.append(bt)
+        nc.scalar.activation(out=warm[:], in_=zero[:], func=ACT.Sigmoid)
+        bias = []
+        for gate in range(2):
+            bs = const.tile([P, J], F32, name="bias%d" % gate)
+            bias.append(bs)
+
+        out0 = const.tile([P, J * B], F32, name="out0")
+        out8 = const.tile([P, J * B], FP8, name="out8")
+        stats = const.tile([P, 8], F32, name="stats")
+        part = const.tile([P, 1], F32, name="part")
+        junk = const.tile([P, P], F32, name="junk")
+        scale = const.tile([P, 1], F32, name="scale")
+        factor = const.tile([P, 1], F32, name="factor")
+        h_raw = const.tile([P, K], BF16, name="h_raw")
+        x_raw = const.tile([P, PASSES, 4, B], BF16, name="x_raw")
+        x_grp = const.tile([P, PASSES, B, 4], BF16, name="x_grp", align_bytes=64)
+        act_codes = []
+        act_scales = []
+        for n in range(2):
+            ac = const.tile([P, PASSES * B], U32, name="act_codes%d" % n, align_bytes=64)
+            asc = const.tile([P, PASSES * B], U8, name="act_scales%d" % n, align_bytes=64)
+            act_codes.append(ac)
+            act_scales.append(asc)
+
+        raws = {}
+        perms = {}
+        banks = {}
+        grps = {}
+        codes = {}
+        accs = {}
+        gates = {}
+
+        def load(ss):
+            jp, gate = ss // 2, ss % 2
+            pair = []
+            for n in range(2):
+                raw = rawp.tile([P, 2, K], BF16, name="raw", tag="raw")
+                pair.append(raw)
+            raws[ss] = pair
+            srcs = (wx[gate], wh[gate])
+            split = load_split(ss)
+            if split == 1:
+                for n in range(2):
+                    nc.sync.dma_start(out=pair[n][:], in_=srcs[n][:, 2 * jp : 2 * jp + 2, :])
+            else:
+                kw = K // (split // 2)
+                for jj in range(2):
+                    for k0 in range(0, K, kw):
+                        for n in range(2):
+                            nc.sync.dma_start(out=pair[n][:, jj, k0 : k0 + kw], in_=srcs[n][:, 2 * jp + jj, k0 : k0 + kw])
+                    if ss == 0 and jj == 0:
+                        nc.sync.dma_start(out=x_raw[:], in_=x.rearrange("(g p t) b -> p g t b", g=PASSES, t=4))
+
+        def words_of(t, n):
+            return raws[t // 2][n][:, t % 2, :].bitcast(F32)
+
+        def permute(t):
+            flags = perm_flags(t)
+            for n in range(2):
+                if flags[n]:
+                    pm = permp.tile([P, WORDS], F32, name="pm", tag="pm")
+                    nc.vector.tensor_copy(
+                        out=pm[:].rearrange("p (g u c) -> p g u c", g=PASSES, u=2),
+                        in_=words_of(t, n).rearrange("p (g c u) -> p g u c", g=PASSES, u=2),
+                    )
+                    perms[(t, n)] = pm
+
+        def transpose_unit(words, pm):
+            res = []
+            for half in range(2):
+                bank = trp.tile([P, 2, 2, P], F32, name="bank", tag="bank")
+                for gg in range(2):
+                    g = 2 * half + gg
+                    for u in range(2):
+                        if pm is None:
+                            src = words[:, 256 * g + u : 256 * (g + 1) : 2]
+                        else:
+                            src = pm[:, 128 * (2 * g + u) : 128 * (2 * g + u + 1)]
+                        nc.tensor.transpose(bank[:, gg, u, :], src, ident[:])
+                res.append(bank)
+            return res
+
+        def evac_unit(two_banks, engines):
+            grp = grpp.tile([P, K], BF16, name="grp", tag="grp", align_bytes=64)
+            gw = grp[:].bitcast(F32)
+            for half in range(2):
+                dst = gw[:, 512 * half : 512 * (half + 1)].rearrange("p (g r u) -> p g r u", g=2, u=2)
+                src = two_banks[half][:].rearrange("p g u r -> p g r u")
+                if engines[half] == "V":
+                    nc.vector.tensor_copy(out=dst, in_=src)
+                else:
+                    nc.scalar.copy(out=dst, in_=src)
+            return grp
+
+        def quantize(grp_ap, cd, sc):
+            nc.vector.quantize_mx(out=cd.bitcast(FP8X4), scales=sc, in_=grp_ap)
+
+        def quant_step(t):
+            pair = []
+            for n in range(2):
+                cd = codep.tile([P, PASSES * P], U32, name="cd", tag="cd", align_bytes=64)
+                sc = codep.tile([P, PASSES * P], U8, name="sc", tag="sc", align_bytes=64)
+                quantize(grps[t][n][:], cd[:], sc[:])
+                pair.append((cd, sc))
+            codes[t] = pair
+
+        def mm_step(t):
+            gate, jj = (t % 4) // 2, t % 2
+            if jj == 0:
+                acc = accp.tile([P, 2, B], F32, name="acc%d" % gate, tag="acc%d" % gate)
+                accs[gate] = acc
+            acc = accs[gate]
+            for n in range(2):
+                cd, sc = codes[t][n]
+                for g in range(PASSES):
+                    cols = slice(P * g, P * (g + 1))
+                    nc.tensor.matmul_mx(
+                        out=acc[:, jj, :],
+                        lhsT=cd[:, cols].bitcast(FP8X4),
+                        lhsT_scale=sc[:, cols],
+                        rhs=act_codes[n][:, cols].bitcast(FP8X4),
+                        rhs_scale=act_scales[n][:, cols],
+                        start=(n == 0 and g == 0),
+                        stop=(n == 1 and g == PASSES - 1),
+                    )
+
+        def act_step(t):
+            jp, gate, jj = t // 4, (t % 4) // 2, t % 2
+            if jj == 0:
+                gt = gatep.tile([P, 2 * B], F32, name="gate%d" % gate, tag="gate%d" % gate)
+                gates[gate] = gt
+            j = 2 * jp + jj
+            nc.scalar.activation(
+                out=gates[gate][:, B * jj : B * (jj + 1)],
+                in_=accs[gate][:, jj, :],
+                func=(ACT.Sigmoid if gate == 0 else ACT.Tanh),
+                bias=bias[gate][:, j : j + 1],
+                scale=1.0,
+            )
+
+        def product(jp):
+            cols = slice(2 * B * jp, 2 * B * (jp + 1))
+            nc.vector.tensor_tensor(out=out0[:, cols], in0=gates[0][:], in1=gates[1][:], op=ALU.mult)
+            nc.vector.tensor_reduce(out=stats[:, jp : jp + 1], in_=out0[:, cols], axis=AX.X, op=ALU.max, apply_absolute_value=True)
+
+        def store0(j0, j1):
+            nc.sync.dma_start(out=out0_v[:, j0:j1, :], in_=out0[:, B * j0 : B * j1].rearrange("p (j b) -> p j b", b=B))
+
+        with tc.manual_schedule():
+            nc.sync.dma_start(out=h_raw[:], in_=h)
+            for ss in range(LOAD_AHEAD):
+                load(ss)
+            for gate in range(2):
+                nc.vector.tensor_tensor(out=bias[gate][:], in0=bias_raw[2 * gate][:], in1=bias_raw[2 * gate + 1][:], op=ALU.add)
+            h_banks = transpose_unit(h_raw[:].bitcast(F32), None)
+            h_grp = evac_unit(h_banks, "SV")
+            permute(0)
+            permute(1)
+            for t in range(STEPS + 4):
+                if t % 2 == 0 and t // 2 + LOAD_AHEAD < STEPS // 2:
+                    load(t // 2 + LOAD_AHEAD)
+                if t < STEPS:
+                    banks[t] = [transpose_unit(words_of(t, n), perms.get((t, n))) for n in range(2)]
+                if 0 <= t - 2 < STEPS:
+                    mm_step(t - 2)
+                if t == 0:
+                    quantize(h_grp[:], act_codes[1][:], act_scales[1][:])
+                if 0 <= t - 1 < STEPS:
+                    quant_step(t - 1)
+                if t >= 3 and (t - 3) % 4 == 3 and t - 3 < STEPS:
+                    product((t - 3) // 4)
+                if t < STEPS:
+                    eng = evac_engines(t)
+                    grps[t] = [evac_unit(banks[t][n], eng[2 * n : 2 * n + 2]) for n in range(2)]
+                if t == 0:
+                    nc.vector.tensor_copy(out=x_grp[:], in_=x_raw[:].rearrange("p g t b -> p g b t"))
+                    quantize(x_grp[:].rearrange("p g b t -> p (g b t)"), act_codes[0][:], act_scales[0][:])
+                if t + 2 < STEPS:
+                    permute(t + 2)
+                if 0 <= t - 2 < STEPS:
+                    act_step(t - 2)
+                if t == STEPS:
+                    store0(0, J - 2)
+
+            store0(J - 2, J)
+            nc.vector.tensor_reduce(out=part[:], in_=stats[:], axis=AX.X, op=ALU.max)
+            spread = trp.tile([P, 2, 2, P], F32, name="bank", tag="bank")
+            nc.tensor.transpose(spread[:, 0, 0, :], part[:, 0:1].to_broadcast([P, P]), ident[:])
+            nc.vector.tensor_scalar(
+                out=junk[:], in0=spread[:, 0, 0, :], scalar1=1.0 / 448.0, scalar2=None, op0=ALU.mult, op1=ALU.max, accum_out=scale[:, 0:1]
+            )
+            nc.vector.reciprocal(out=factor[:], in_=scale[:])
+            nc.vector.tensor_scalar(
+                out=out8[:, 0:V_CAST], in0=out0[:, 0:V_CAST], scalar1=factor[:, 0:1], scalar2=None, op0=ALU.mult, saturate=False
+            )
+            nc.scalar.activation(
+                out=out8[:, V_CAST:], in_=out0[:, V_CAST:], func=ACT.Identity, scale=factor[:, 0:1], bias=zero[:, 0:1], saturate=False
+            )
+            jv = V_CAST // B
+            bytes8 = out8[:].bitcast(U8).rearrange("p (j b) -> p j b", b=B)
+            nc.sync.dma_start(out=out1_v[:, 0:jv, :], in_=bytes8[:, 0:jv, :])
+            nc.sync.dma_start(out=out1_v[:, jv:J, :], in_=bytes8[:, jv:J, :])

@@ -28,11 +28,11 @@ V_CAST = 1408
 
 
 def perm_flags(t):
-    return (False, False)
+    return (True, t % 2 == 1)
 
 
 def evac_engines(t):
-    return "SSSV"
+    return "SSSV" if t % 4 == 0 or t == STEPS - 1 else "SSSS"
 
 
 def load_split(ss):

@@ -22,21 +22,25 @@ J = 16
 WORDS = K // 2
 PASSES = 4
 STEPS = 32
-RAW_BUFS = 10
-LOAD_AHEAD = RAW_BUFS // 2 - 1
+RAW_BUFS = 5
+LOAD_AHEAD = RAW_BUFS - 1
 V_CAST = 1408
 
 
-def perm_flags(t):
-    return (True, t % 2 == 1)
+def perm_count(t):
+    return 1
 
 
 def evac_engines(t):
-    return "SSSV" if t % 4 == 0 or t == STEPS - 1 else "SSSS"
+    return "SVSS" if t == STEPS - 1 else ("SSSV" if t % 2 == 0 else "SSSS")
 
 
 def load_split(ss):
-    return 2 if ss == 0 or ss == STEPS // 2 - 1 else 1
+    return 2 if ss <= 1 or ss == STEPS // 2 - 1 else 1
+
+
+def quant_pieces(t):
+    return (2, 1, 1) if t == STEPS - 1 else ((2, 2) if t == STEPS - 2 else (4,))
 
 
 def tile_naivelstm_pa_kernel(tc, x, h, w_ii, w_ig, w_hi, w_hg, b_ii, b_hi, b_ig, b_hg, out_0, out_1):
@@ -49,9 +53,9 @@ def tile_naivelstm_pa_kernel(tc, x, h, w_ii, w_ig, w_hi, w_hg, b_ii, b_hi, b_ig,
     with ExitStack() as ctx:
         const = ctx.enter_context(tc.tile_pool(name="const", bufs=1))
         rawp = ctx.enter_context(tc.tile_pool(name="rawp", bufs=RAW_BUFS))
-        permp = ctx.enter_context(tc.tile_pool(name="permp", bufs=8))
-        grpp = ctx.enter_context(tc.tile_pool(name="grpp", bufs=6))
-        codep = ctx.enter_context(tc.tile_pool(name="codep", bufs=6))
+        permp = ctx.enter_context(tc.tile_pool(name="permp", bufs=4))
+        grpp = ctx.enter_context(tc.tile_pool(name="grpp", bufs=3))
+        codep = ctx.enter_context(tc.tile_pool(name="codep", bufs=3))
         gatep = ctx.enter_context(tc.tile_pool(name="gatep", bufs=2))
         trp = ctx.enter_context(tc.psum_pool(name="trp", bufs=6))
         accp = ctx.enter_context(tc.psum_pool(name="accp", bufs=1))
@@ -73,14 +77,14 @@ def tile_naivelstm_pa_kernel(tc, x, h, w_ii, w_ig, w_hi, w_hg, b_ii, b_hi, b_ig,
             bs = const.tile([P, J], F32, name="bias%d" % gate)
             bias.append(bs)
 
-        out0 = const.tile([P, J * B], F32, name="out0")
+        out0 = const.tile([P, J * B + 8], F32, name="out0")
         out8 = const.tile([P, J * B], FP8, name="out8")
-        stats = const.tile([P, 8], F32, name="stats")
         part = const.tile([P, 1], F32, name="part")
         junk = const.tile([P, P], F32, name="junk")
         scale = const.tile([P, 1], F32, name="scale")
         factor = const.tile([P, 1], F32, name="factor")
         h_raw = const.tile([P, K], BF16, name="h_raw")
+        h_grp = const.tile([P, K], BF16, name="h_grp", align_bytes=64)
         x_raw = const.tile([P, PASSES, 4, B], BF16, name="x_raw")
         x_grp = const.tile([P, PASSES, B, 4], BF16, name="x_grp", align_bytes=64)
         act_codes = []
@@ -101,38 +105,34 @@ def tile_naivelstm_pa_kernel(tc, x, h, w_ii, w_ig, w_hi, w_hg, b_ii, b_hi, b_ig,
 
         def load(ss):
             jp, gate = ss // 2, ss % 2
-            pair = []
-            for n in range(2):
-                raw = rawp.tile([P, 2, K], BF16, name="raw", tag="raw")
-                pair.append(raw)
-            raws[ss] = pair
+            raw = rawp.tile([P, 2, 2, K], BF16, name="raw", tag="raw")
+            raws[ss] = raw
             srcs = (wx[gate], wh[gate])
             split = load_split(ss)
             if split == 1:
                 for n in range(2):
-                    nc.sync.dma_start(out=pair[n][:], in_=srcs[n][:, 2 * jp : 2 * jp + 2, :])
+                    nc.sync.dma_start(out=raw[:, :, n, :], in_=srcs[n][:, 2 * jp : 2 * jp + 2, :])
             else:
                 kw = K // (split // 2)
                 for jj in range(2):
-                    for k0 in range(0, K, kw):
-                        for n in range(2):
-                            nc.sync.dma_start(out=pair[n][:, jj, k0 : k0 + kw], in_=srcs[n][:, 2 * jp + jj, k0 : k0 + kw])
+                    for n in range(2):
+                        for k0 in range(0, K, kw):
+                            nc.sync.dma_start(out=raw[:, jj, n, k0 : k0 + kw], in_=srcs[n][:, 2 * jp + jj, k0 : k0 + kw])
                     if ss == 0 and jj == 0:
                         nc.sync.dma_start(out=x_raw[:], in_=x.rearrange("(g p t) b -> p g t b", g=PASSES, t=4))
 
-        def words_of(t, n):
-            return raws[t // 2][n][:, t % 2, :].bitcast(F32)
+        def words_of(t):
+            return raws[t // 2][:, t % 2, :, :].rearrange("p n k -> p (n k)").bitcast(F32)
 
         def permute(t):
-            flags = perm_flags(t)
-            for n in range(2):
-                if flags[n]:
-                    pm = permp.tile([P, WORDS], F32, name="pm", tag="pm")
-                    nc.vector.tensor_copy(
-                        out=pm[:].rearrange("p (g u c) -> p g u c", g=PASSES, u=2),
-                        in_=words_of(t, n).rearrange("p (g c u) -> p g u c", g=PASSES, u=2),
-                    )
-                    perms[(t, n)] = pm
+            cnt = perm_count(t)
+            if cnt > 0:
+                pm = permp.tile([P, 2 * WORDS], F32, name="pm", tag="pm")
+                nc.vector.tensor_copy(
+                    out=pm[:, 0 : cnt * WORDS].rearrange("p (g u c) -> p g u c", g=cnt * PASSES, u=2),
+                    in_=words_of(t)[:, 0 : cnt * WORDS].rearrange("p (g c u) -> p g u c", g=cnt * PASSES, u=2),
+                )
+                perms[t] = pm
 
         def transpose_unit(words, pm):
             res = []
@@ -149,29 +149,43 @@ def tile_naivelstm_pa_kernel(tc, x, h, w_ii, w_ig, w_hi, w_hg, b_ii, b_hi, b_ig,
                 res.append(bank)
             return res
 
-        def evac_unit(two_banks, engines):
-            grp = grpp.tile([P, K], BF16, name="grp", tag="grp", align_bytes=64)
-            gw = grp[:].bitcast(F32)
-            for half in range(2):
-                dst = gw[:, 512 * half : 512 * (half + 1)].rearrange("p (g r u) -> p g r u", g=2, u=2)
-                src = two_banks[half][:].rearrange("p g u r -> p g r u")
-                if engines[half] == "V":
+        def transpose_step(t):
+            res = []
+            words = words_of(t)
+            for n in range(2):
+                if n < perm_count(t):
+                    res.extend(transpose_unit(None, perms[t][:, n * WORDS : (n + 1) * WORDS]))
+                else:
+                    res.extend(transpose_unit(words[:, n * WORDS : (n + 1) * WORDS], None))
+            banks[t] = res
+
+        def evac(bank_list, engines, grp_ap):
+            gw = grp_ap.bitcast(F32)
+            for b in range(len(bank_list)):
+                dst = gw[:, 512 * b : 512 * (b + 1)].rearrange("p (g r u) -> p g r u", g=2, u=2)
+                src = bank_list[b][:].rearrange("p g u r -> p g r u")
+                if engines[b] == "V":
                     nc.vector.tensor_copy(out=dst, in_=src)
                 else:
                     nc.scalar.copy(out=dst, in_=src)
-            return grp
+
+        def evac_step(t):
+            grp = grpp.tile([P, 2 * K], BF16, name="grp", tag="grp", align_bytes=64)
+            grps[t] = grp
+            evac(banks[t], evac_engines(t), grp[:])
 
         def quantize(grp_ap, cd, sc):
             nc.vector.quantize_mx(out=cd.bitcast(FP8X4), scales=sc, in_=grp_ap)
 
         def quant_step(t):
-            pair = []
-            for n in range(2):
-                cd = codep.tile([P, PASSES * P], U32, name="cd", tag="cd", align_bytes=64)
-                sc = codep.tile([P, PASSES * P], U8, name="sc", tag="sc", align_bytes=64)
-                quantize(grps[t][n][:], cd[:], sc[:])
-                pair.append((cd, sc))
-            codes[t] = pair
+            cd = codep.tile([P, 2 * PASSES * P], U32, name="cd", tag="cd", align_bytes=64)
+            sc = codep.tile([P, 2 * PASSES * P], U8, name="sc", tag="sc", align_bytes=64)
+            codes[t] = (cd, sc)
+            c0 = 0
+            for nbanks in quant_pieces(t):
+                c1 = c0 + 2 * P * nbanks
+                quantize(grps[t][:, 4 * c0 : 4 * c1], cd[:, c0:c1], sc[:, c0:c1])
+                c0 = c1
 
         def mm_step(t):
             gate, jj = (t % 4) // 2, t % 2
@@ -179,16 +193,17 @@ def tile_naivelstm_pa_kernel(tc, x, h, w_ii, w_ig, w_hi, w_hg, b_ii, b_hi, b_ig,
                 acc = accp.tile([P, 2, B], F32, name="acc%d" % gate, tag="acc%d" % gate)
                 accs[gate] = acc
             acc = accs[gate]
+            cd, sc = codes[t]
             for n in range(2):
-                cd, sc = codes[t][n]
                 for g in range(PASSES):
-                    cols = slice(P * g, P * (g + 1))
+                    wcols = slice(P * (PASSES * n + g), P * (PASSES * n + g + 1))
+                    acols = slice(B * g, B * (g + 1))
                     nc.tensor.matmul_mx(
                         out=acc[:, jj, :],
-                        lhsT=cd[:, cols].bitcast(FP8X4),
-                        lhsT_scale=sc[:, cols],
-                        rhs=act_codes[n][:, cols].bitcast(FP8X4),
-                        rhs_scale=act_scales[n][:, cols],
+                        lhsT=cd[:, wcols].bitcast(FP8X4),
+                        lhsT_scale=sc[:, wcols],
+                        rhs=act_codes[n][:, acols].bitcast(FP8X4),
+                        rhs_scale=act_scales[n][:, acols],
                         start=(n == 0 and g == 0),
                         stop=(n == 1 and g == PASSES - 1),
                     )
@@ -207,10 +222,13 @@ def tile_naivelstm_pa_kernel(tc, x, h, w_ii, w_ig, w_hi, w_hg, b_ii, b_hi, b_ig,
                 scale=1.0,
             )
 
-        def product(jp):
-            cols = slice(2 * B * jp, 2 * B * (jp + 1))
-            nc.vector.tensor_tensor(out=out0[:, cols], in0=gates[0][:], in1=gates[1][:], op=ALU.mult)
-            nc.vector.tensor_reduce(out=stats[:, jp : jp + 1], in_=out0[:, cols], axis=AX.X, op=ALU.max, apply_absolute_value=True)
+        def product(j0, j1):
+            g0 = B * (j0 % 2)
+            g1 = g0 + B * (j1 - j0)
+            nc.vector.tensor_tensor(out=out0[:, B * j0 : B * j1], in0=gates[0][:, g0:g1], in1=gates[1][:, g0:g1], op=ALU.mult)
+
+        def abs_max(c0, c1, dst):
+            nc.vector.tensor_reduce(out=dst, in_=out0[:, c0:c1], axis=AX.X, op=ALU.max, apply_absolute_value=True)
 
         def store0(j0, j1):
             nc.sync.dma_start(out=out0_v[:, j0:j1, :], in_=out0[:, B * j0 : B * j1].rearrange("p (j b) -> p j b", b=B))
@@ -222,25 +240,32 @@ def tile_naivelstm_pa_kernel(tc, x, h, w_ii, w_ig, w_hi, w_hg, b_ii, b_hi, b_ig,
             for gate in range(2):
                 nc.vector.tensor_tensor(out=bias[gate][:], in0=bias_raw[2 * gate][:], in1=bias_raw[2 * gate + 1][:], op=ALU.add)
             h_banks = transpose_unit(h_raw[:].bitcast(F32), None)
-            h_grp = evac_unit(h_banks, "SV")
+            evac(h_banks, "SV", h_grp[:])
             permute(0)
             permute(1)
             for t in range(STEPS + 4):
                 if t % 2 == 0 and t // 2 + LOAD_AHEAD < STEPS // 2:
                     load(t // 2 + LOAD_AHEAD)
                 if t < STEPS:
-                    banks[t] = [transpose_unit(words_of(t, n), perms.get((t, n))) for n in range(2)]
+                    transpose_step(t)
                 if 0 <= t - 2 < STEPS:
                     mm_step(t - 2)
                 if t == 0:
                     quantize(h_grp[:], act_codes[1][:], act_scales[1][:])
                 if 0 <= t - 1 < STEPS:
                     quant_step(t - 1)
-                if t >= 3 and (t - 3) % 4 == 3 and t - 3 < STEPS:
-                    product((t - 3) // 4)
+                if t >= 4 and (t - 4) % 4 == 3 and t - 4 < STEPS - 4:
+                    jp = (t - 4) // 4
+                    abs_max(2 * B * jp, 2 * B * (jp + 1), out0[:, J * B + jp : J * B + jp + 1])
+                if t >= 3 and (t - 3) % 4 == 3 and t - 3 < STEPS - 4:
+                    product(2 * ((t - 3) // 4), 2 * ((t - 3) // 4) + 2)
+                if t - 3 == STEPS - 2:
+                    product(J - 2, J - 1)
+                if t - 3 == STEPS - 1:
+                    abs_max(B * (J - 2), B * (J - 1), out0[:, J * B + 7 : J * B + 8])
+                    product(J - 1, J)
                 if t < STEPS:
-                    eng = evac_engines(t)
-                    grps[t] = [evac_unit(banks[t][n], eng[2 * n : 2 * n + 2]) for n in range(2)]
+                    evac_step(t)
                 if t == 0:
                     nc.vector.tensor_copy(out=x_grp[:], in_=x_raw[:].rearrange("p g t b -> p g b t"))
                     quantize(x_grp[:].rearrange("p g b t -> p (g b t)"), act_codes[0][:], act_scales[0][:])
@@ -251,8 +276,8 @@ def tile_naivelstm_pa_kernel(tc, x, h, w_ii, w_ig, w_hi, w_hg, b_ii, b_hi, b_ig,
                 if t == STEPS:
                     store0(0, J - 2)
 
+            abs_max(B * (J - 1), J * B + 8, part[:, 0:1])
             store0(J - 2, J)
-            nc.vector.tensor_reduce(out=part[:], in_=stats[:], axis=AX.X, op=ALU.max)
             spread = trp.tile([P, 2, 2, P], F32, name="bank", tag="bank")
             nc.tensor.transpose(spread[:, 0, 0, :], part[:, 0:1].to_broadcast([P, P]), ident[:])
             nc.vector.tensor_scalar(
@@ -263,7 +288,7 @@ def tile_naivelstm_pa_kernel(tc, x, h, w_ii, w_ig, w_hi, w_hg, b_ii, b_hi, b_ig,
                 out=out8[:, 0:V_CAST], in0=out0[:, 0:V_CAST], scalar1=factor[:, 0:1], scalar2=None, op0=ALU.mult, saturate=False
             )
             nc.scalar.activation(
-                out=out8[:, V_CAST:], in_=out0[:, V_CAST:], func=ACT.Identity, scale=factor[:, 0:1], bias=zero[:, 0:1], saturate=False
+                out=out8[:, V_CAST:], in_=out0[:, V_CAST : J * B], func=ACT.Identity, scale=factor[:, 0:1], bias=zero[:, 0:1], saturate=False
             )
             jv = V_CAST // B
             bytes8 = out8[:].bitcast(U8).rearrange("p (j b) -> p j b", b=B)

@@ -28,7 +28,7 @@ V_CAST = 1408
 
 
 def perm_count(t):
-    return 1
+    return 0 if t < 3 else 1
 
 
 def evac_engines(t):
@@ -36,7 +36,7 @@ def evac_engines(t):
 
 
 def load_split(ss):
-    return 2 if ss <= 1 or ss == STEPS // 2 - 1 else 1
+    return 2 if ss <= 4 or ss == STEPS // 2 - 1 else 1
 
 
 def quant_pieces(t):
@@ -234,7 +234,8 @@ def tile_naivelstm_pa_kernel(tc, x, h, w_ii, w_ig, w_hi, w_hg, b_ii, b_hi, b_ig,
             nc.sync.dma_start(out=out0_v[:, j0:j1, :], in_=out0[:, B * j0 : B * j1].rearrange("p (j b) -> p j b", b=B))
 
         with tc.manual_schedule():
-            nc.sync.dma_start(out=h_raw[:], in_=h)
+            for k0 in range(0, K, K // 2):
+                nc.sync.dma_start(out=h_raw[:, k0 : k0 + K // 2], in_=h[:, k0 : k0 + K // 2])
             for ss in range(LOAD_AHEAD):
                 load(ss)
             for gate in range(2):

@@ -244,39 +244,48 @@ def tile_naivelstm_pa_kernel(tc, x, h, w_ii, w_ig, w_hi, w_hg, b_ii, b_hi, b_ig,
             evac(h_banks, "SV", h_grp[:])
             permute(0)
             permute(1)
-            for t in range(STEPS + 4):
-                if t % 2 == 0 and t // 2 + LOAD_AHEAD < STEPS // 2:
-                    load(t // 2 + LOAD_AHEAD)
-                if t < STEPS:
-                    transpose_step(t)
-                if 0 <= t - 2 < STEPS:
-                    mm_step(t - 2)
-                if t == 0:
+            for d in range(STEPS // 2 + 1):
+                t0 = 2 * d
+                t1 = t0 + 1
+                if d + LOAD_AHEAD < STEPS // 2:
+                    load(d + LOAD_AHEAD)
+                if t0 < STEPS:
+                    transpose_step(t0)
+                if d == 0:
                     quantize(h_grp[:], act_codes[1][:], act_scales[1][:])
-                if 0 <= t - 1 < STEPS:
-                    quant_step(t - 1)
-                if t >= 4 and (t - 4) % 4 == 3 and t - 4 < STEPS - 4:
-                    jp = (t - 4) // 4
-                    abs_max(2 * B * jp, 2 * B * (jp + 1), out0[:, J * B + jp : J * B + jp + 1])
-                if t >= 3 and (t - 3) % 4 == 3 and t - 3 < STEPS - 4:
-                    product(2 * ((t - 3) // 4), 2 * ((t - 3) // 4) + 2)
-                if t - 3 == STEPS - 2:
-                    product(J - 2, J - 1)
-                if t - 3 == STEPS - 1:
-                    abs_max(B * (J - 2), B * (J - 1), out0[:, J * B + 7 : J * B + 8])
-                    product(J - 1, J)
-                if t < STEPS:
-                    evac_step(t)
-                if t == 0:
+                if d > 0:
+                    quant_step(t0 - 1)
+                if t0 < STEPS:
+                    evac_step(t0)
+                if d == 0:
                     nc.vector.tensor_copy(out=x_grp[:], in_=x_raw[:].rearrange("p g t b -> p g b t"))
                     quantize(x_grp[:].rearrange("p g b t -> p (g b t)"), act_codes[0][:], act_scales[0][:])
-                if t + 2 < STEPS:
-                    permute(t + 2)
-                if 0 <= t - 2 < STEPS:
-                    act_step(t - 2)
-                if t == STEPS:
-                    store0(0, J - 2)
-
+                if t0 + 2 < STEPS:
+                    permute(t0 + 2)
+                if t1 < STEPS:
+                    transpose_step(t1)
+                    quant_step(t0)
+                if d >= 3 and d % 2 == 1:
+                    product(d - 3, d - 1)
+                if t1 < STEPS:
+                    evac_step(t1)
+                if t1 + 2 < STEPS:
+                    permute(t1 + 2)
+                if d >= 4 and d % 2 == 0:
+                    abs_max(B * (d - 4), B * (d - 2), out0[:, J * B + (d - 4) // 2 : J * B + (d - 4) // 2 + 1])
+                if 0 < d < STEPS // 2:
+                    mm_step(t0 - 2)
+                    mm_step(t0 - 1)
+                    act_step(t0 - 2)
+                    act_step(t0 - 1)
+            store0(0, J - 2)
+            mm_step(STEPS - 2)
+            act_step(STEPS - 2)
+            mm_step(STEPS - 1)
+            act_step(STEPS - 1)
+            product(J - 2, J - 1)
+            abs_max(B * (J - 2), B * (J - 1), out0[:, J * B + 7 : J * B + 8])
+            product(J - 1, J)
             abs_max(B * (J - 1), J * B + 8, part[:, 0:1])
             store0(J - 2, J)
             spread = trp.tile([P, 2, 2, P], F32, name="bank", tag="bank")

@@ -28,7 +28,7 @@ V_CAST = 1408
 
 
 def perm_count(t):
-    return 0 if t < 3 else 1
+    return 0 if t < 3 else (2 if t % 4 == 3 else 1)
 
 
 def evac_engines(t):

@@ -32,7 +32,7 @@ def perm_count(t):
 
 
 def evac_engines(t):
-    return "SVSS" if t == STEPS - 1 else ("SSSV" if t % 2 == 0 else "SSSS")
+    return "SVSS" if t == STEPS - 1 else ("SSSV" if t % 4 == 0 else "SSSS")
 
 
 def load_split(ss):

@@ -129,8 +129,8 @@ def tile_naivelstm_pa_kernel(tc, x, h, w_ii, w_ig, w_hi, w_hg, b_ii, b_hi, b_ig,
             if cnt > 0:
                 pm = permp.tile([P, 2 * WORDS], F32, name="pm", tag="pm")
                 nc.vector.tensor_copy(
-                    out=pm[:, 0 : cnt * WORDS].rearrange("p (g u c) -> p g u c", g=cnt * PASSES, u=2),
-                    in_=words_of(t)[:, 0 : cnt * WORDS].rearrange("p (g c u) -> p g u c", g=cnt * PASSES, u=2),
+                    out=pm[:].rearrange("p (u m i) -> p m u i", u=2, i=4)[:, 0 : cnt * WORDS // 8, :, :],
+                    in_=words_of(t)[:, 0 : cnt * WORDS].rearrange("p (m i u) -> p m u i", i=4, u=2),
                 )
                 perms[t] = pm
 
@@ -144,7 +144,7 @@ def tile_naivelstm_pa_kernel(tc, x, h, w_ii, w_ig, w_hi, w_hg, b_ii, b_hi, b_ig,
                         if pm is None:
                             src = words[:, 256 * g + u : 256 * (g + 1) : 2]
                         else:
-                            src = pm[:, 128 * (2 * g + u) : 128 * (2 * g + u + 1)]
+                            src = pm[:, WORDS * u + 128 * g : WORDS * u + 128 * (g + 1)]
                         nc.tensor.transpose(bank[:, gg, u, :], src, ident[:])
                 res.append(bank)
             return res
@@ -154,7 +154,7 @@ def tile_naivelstm_pa_kernel(tc, x, h, w_ii, w_ig, w_hi, w_hg, b_ii, b_hi, b_ig,
             words = words_of(t)
             for n in range(2):
                 if n < perm_count(t):
-                    res.extend(transpose_unit(None, perms[t][:, n * WORDS : (n + 1) * WORDS]))
+                    res.extend(transpose_unit(None, perms[t][:, n * WORDS // 2 : 2 * WORDS]))
                 else:
                     res.extend(transpose_unit(words[:, n * WORDS : (n + 1) * WORDS], None))
             banks[t] = res

@@ -28,7 +28,7 @@ V_CAST = 1408
 
 
 def perm_count(t):
-    return 0 if t < 3 else (2 if t % 4 == 3 else 1)
+    return 0 if t < 4 else (2 if t % 4 == 3 else 1)
 
 
 def evac_engines(t):

from contextlib import ExitStack

import concourse.mybir as mybir
from concourse.masks import make_identity

FLOPS = 4 * 2 * 2048 * 2048 * 128

F32 = mybir.dt.float32
BF16 = mybir.dt.bfloat16
U32 = mybir.dt.uint32
U8 = mybir.dt.uint8
FP8X4 = mybir.dt.float8_e4m3fn_x4
FP8 = mybir.dt.float8_e4m3fn
ALU = mybir.AluOpType
ACT = mybir.ActivationFunctionType
AX = mybir.AxisListType

P = 128
K = 2048
B = 128
J = 16
WORDS = K // 2
PASSES = 4
STEPS = 32
RAW_BUFS = 5
LOAD_AHEAD = RAW_BUFS - 1
V_CAST = 1408


def perm_count(t):
    return 0 if t < 4 else (2 if t % 4 == 3 else 1)


def evac_engines(t):
    return "SVSS" if t == STEPS - 1 else ("SSSV" if t % 4 == 0 else "SSSS")


def load_split(ss):
    return 2 if ss <= 4 or ss == STEPS // 2 - 1 else 1


def quant_pieces(t):
    return (2, 1, 1) if t == STEPS - 1 else ((2, 2) if t == STEPS - 2 else (4,))


def tile_naivelstm_pa_kernel(tc, x, h, w_ii, w_ig, w_hi, w_hg, b_ii, b_hi, b_ig, b_hg, out_0, out_1):
    nc = tc.nc
    wx = [w_ii.rearrange("(p j) k -> p j k", j=J), w_ig.rearrange("(p j) k -> p j k", j=J)]
    wh = [w_hi.rearrange("(p j) k -> p j k", j=J), w_hg.rearrange("(p j) k -> p j k", j=J)]
    out0_v = out_0.rearrange("(p j) b -> p j b", j=J)
    out1_v = out_1.rearrange("(p j) b -> p j b", j=J)

    with ExitStack() as ctx:
        const = ctx.enter_context(tc.tile_pool(name="const", bufs=1))
        rawp = ctx.enter_context(tc.tile_pool(name="rawp", bufs=RAW_BUFS))
        permp = ctx.enter_context(tc.tile_pool(name="permp", bufs=4))
        grpp = ctx.enter_context(tc.tile_pool(name="grpp", bufs=3))
        codep = ctx.enter_context(tc.tile_pool(name="codep", bufs=3))
        gatep = ctx.enter_context(tc.tile_pool(name="gatep", bufs=2))
        trp = ctx.enter_context(tc.psum_pool(name="trp", bufs=6))
        accp = ctx.enter_context(tc.psum_pool(name="accp", bufs=1))

        ident = const.tile([P, P], F32, name="ident")
        make_identity(nc, ident[:])
        zero = const.tile([P, 1], F32, name="zero")
        nc.vector.memset(zero[:], 0.0)
        warm = const.tile([P, 1], F32, name="warm")

        bias_raw = []
        for n, b_ap in enumerate((b_ii, b_hi, b_ig, b_hg)):
            bt = const.tile([P, J], BF16, name="bias_raw%d" % n)
            nc.scalar.dma_start(out=bt[:], in_=b_ap.rearrange("(p j) o -> p (j o)", j=J))
            bias_raw.append(bt)
        nc.scalar.activation(out=warm[:], in_=zero[:], func=ACT.Sigmoid)
        bias = []
        for gate in range(2):
            bs = const.tile([P, J], F32, name="bias%d" % gate)
            bias.append(bs)

        out0 = const.tile([P, J * B + 8], F32, name="out0")
        out8 = const.tile([P, J * B], FP8, name="out8")
        part = const.tile([P, 1], F32, name="part")
        junk = const.tile([P, P], F32, name="junk")
        scale = const.tile([P, 1], F32, name="scale")
        factor = const.tile([P, 1], F32, name="factor")
        h_raw = const.tile([P, K], BF16, name="h_raw")
        h_grp = const.tile([P, K], BF16, name="h_grp", align_bytes=64)
        x_raw = const.tile([P, PASSES, 4, B], BF16, name="x_raw")
        x_grp = const.tile([P, PASSES, B, 4], BF16, name="x_grp", align_bytes=64)
        act_codes = []
        act_scales = []
        for n in range(2):
            ac = const.tile([P, PASSES * B], U32, name="act_codes%d" % n, align_bytes=64)
            asc = const.tile([P, PASSES * B], U8, name="act_scales%d" % n, align_bytes=64)
            act_codes.append(ac)
            act_scales.append(asc)

        raws = {}
        perms = {}
        banks = {}
        grps = {}
        codes = {}
        accs = {}
        gates = {}

        def load(ss):
            jp, gate = ss // 2, ss % 2
            raw = rawp.tile([P, 2, 2, K], BF16, name="raw", tag="raw")
            raws[ss] = raw
            srcs = (wx[gate], wh[gate])
            split = load_split(ss)
            if split == 1:
                for n in range(2):
                    nc.sync.dma_start(out=raw[:, :, n, :], in_=srcs[n][:, 2 * jp : 2 * jp + 2, :])
            else:
                kw = K // (split // 2)
                for jj in range(2):
                    for n in range(2):
                        for k0 in range(0, K, kw):
                            nc.sync.dma_start(out=raw[:, jj, n, k0 : k0 + kw], in_=srcs[n][:, 2 * jp + jj, k0 : k0 + kw])
                    if ss == 0 and jj == 0:
                        nc.sync.dma_start(out=x_raw[:], in_=x.rearrange("(g p t) b -> p g t b", g=PASSES, t=4))

        def words_of(t):
            return raws[t // 2][:, t % 2, :, :].rearrange("p n k -> p (n k)").bitcast(F32)

        def permute(t):
            cnt = perm_count(t)
            if cnt > 0:
                pm = permp.tile([P, 2 * WORDS], F32, name="pm", tag="pm")
                nc.vector.tensor_copy(
                    out=pm[:].rearrange("p (u m i) -> p m u i", u=2, i=4)[:, 0 : cnt * WORDS // 8, :, :],
                    in_=words_of(t)[:, 0 : cnt * WORDS].rearrange("p (m i u) -> p m u i", i=4, u=2),
                )
                perms[t] = pm

        def transpose_unit(words, pm):
            res = []
            for half in range(2):
                bank = trp.tile([P, 2, 2, P], F32, name="bank", tag="bank")
                for gg in range(2):
                    g = 2 * half + gg
                    for u in range(2):
                        if pm is None:
                            src = words[:, 256 * g + u : 256 * (g + 1) : 2]
                        else:
                            src = pm[:, WORDS * u + 128 * g : WORDS * u + 128 * (g + 1)]
                        nc.tensor.transpose(bank[:, gg, u, :], src, ident[:])
                res.append(bank)
            return res

        def transpose_step(t):
            res = []
            words = words_of(t)
            for n in range(2):
                if n < perm_count(t):
                    res.extend(transpose_unit(None, perms[t][:, n * WORDS // 2 : 2 * WORDS]))
                else:
                    res.extend(transpose_unit(words[:, n * WORDS : (n + 1) * WORDS], None))
            banks[t] = res

        def evac(bank_list, engines, grp_ap):
            gw = grp_ap.bitcast(F32)
            for b in range(len(bank_list)):
                dst = gw[:, 512 * b : 512 * (b + 1)].rearrange("p (g r u) -> p g r u", g=2, u=2)
                src = bank_list[b][:].rearrange("p g u r -> p g r u")
                if engines[b] == "V":
                    nc.vector.tensor_copy(out=dst, in_=src)
                else:
                    nc.scalar.copy(out=dst, in_=src)

        def evac_step(t):
            grp = grpp.tile([P, 2 * K], BF16, name="grp", tag="grp", align_bytes=64)
            grps[t] = grp
            evac(banks[t], evac_engines(t), grp[:])

        def quantize(grp_ap, cd, sc):
            nc.vector.quantize_mx(out=cd.bitcast(FP8X4), scales=sc, in_=grp_ap)

        def quant_step(t):
            cd = codep.tile([P, 2 * PASSES * P], U32, name="cd", tag="cd", align_bytes=64)
            sc = codep.tile([P, 2 * PASSES * P], U8, name="sc", tag="sc", align_bytes=64)
            codes[t] = (cd, sc)
            c0 = 0
            for nbanks in quant_pieces(t):
                c1 = c0 + 2 * P * nbanks
                quantize(grps[t][:, 4 * c0 : 4 * c1], cd[:, c0:c1], sc[:, c0:c1])
                c0 = c1

        def mm_step(t):
            gate, jj = (t % 4) // 2, t % 2
            if jj == 0:
                acc = accp.tile([P, 2, B], F32, name="acc%d" % gate, tag="acc%d" % gate)
                accs[gate] = acc
            acc = accs[gate]
            cd, sc = codes[t]
            for n in range(2):
                for g in range(PASSES):
                    wcols = slice(P * (PASSES * n + g), P * (PASSES * n + g + 1))
                    acols = slice(B * g, B * (g + 1))
                    nc.tensor.matmul_mx(
                        out=acc[:, jj, :],
                        lhsT=cd[:, wcols].bitcast(FP8X4),
                        lhsT_scale=sc[:, wcols],
                        rhs=act_codes[n][:, acols].bitcast(FP8X4),
                        rhs_scale=act_scales[n][:, acols],
                        start=(n == 0 and g == 0),
                        stop=(n == 1 and g == PASSES - 1),
                    )

        def act_step(t):
            jp, gate, jj = t // 4, (t % 4) // 2, t % 2
            if jj == 0:
                gt = gatep.tile([P, 2 * B], F32, name="gate%d" % gate, tag="gate%d" % gate)
                gates[gate] = gt
            j = 2 * jp + jj
            nc.scalar.activation(
                out=gates[gate][:, B * jj : B * (jj + 1)],
                in_=accs[gate][:, jj, :],
                func=(ACT.Sigmoid if gate == 0 else ACT.Tanh),
                bias=bias[gate][:, j : j + 1],
                scale=1.0,
            )

        def product(j0, j1):
            g0 = B * (j0 % 2)
            g1 = g0 + B * (j1 - j0)
            nc.vector.tensor_tensor(out=out0[:, B * j0 : B * j1], in0=gates[0][:, g0:g1], in1=gates[1][:, g0:g1], op=ALU.mult)

        def abs_max(c0, c1, dst):
            nc.vector.tensor_reduce(out=dst, in_=out0[:, c0:c1], axis=AX.X, op=ALU.max, apply_absolute_value=True)

        def store0(j0, j1):
            nc.sync.dma_start(out=out0_v[:, j0:j1, :], in_=out0[:, B * j0 : B * j1].rearrange("p (j b) -> p j b", b=B))

        with tc.manual_schedule():
            for k0 in range(0, K, K // 2):
                nc.sync.dma_start(out=h_raw[:, k0 : k0 + K // 2], in_=h[:, k0 : k0 + K // 2])
            for ss in range(LOAD_AHEAD):
                load(ss)
            for gate in range(2):
                nc.vector.tensor_tensor(out=bias[gate][:], in0=bias_raw[2 * gate][:], in1=bias_raw[2 * gate + 1][:], op=ALU.add)
            h_banks = transpose_unit(h_raw[:].bitcast(F32), None)
            evac(h_banks, "SV", h_grp[:])
            permute(0)
            permute(1)
            for d in range(STEPS // 2 + 1):
                t0 = 2 * d
                t1 = t0 + 1
                if d + LOAD_AHEAD < STEPS // 2:
                    load(d + LOAD_AHEAD)
                if t0 < STEPS:
                    transpose_step(t0)
                if d == 0:
                    quantize(h_grp[:], act_codes[1][:], act_scales[1][:])
                if d > 0:
                    quant_step(t0 - 1)
                if t0 < STEPS:
                    evac_step(t0)
                if d == 0:
                    nc.vector.tensor_copy(out=x_grp[:], in_=x_raw[:].rearrange("p g t b -> p g b t"))
                    quantize(x_grp[:].rearrange("p g b t -> p (g b t)"), act_codes[0][:], act_scales[0][:])
                if t0 + 2 < STEPS:
                    permute(t0 + 2)
                if t1 < STEPS:
                    transpose_step(t1)
                    quant_step(t0)
                if d >= 3 and d % 2 == 1:
                    product(d - 3, d - 1)
                if t1 < STEPS:
                    evac_step(t1)
                if t1 + 2 < STEPS:
                    permute(t1 + 2)
                if d >= 4 and d % 2 == 0:
                    abs_max(B * (d - 4), B * (d - 2), out0[:, J * B + (d - 4) // 2 : J * B + (d - 4) // 2 + 1])
                if 0 < d < STEPS // 2:
                    mm_step(t0 - 2)
                    mm_step(t0 - 1)
                    act_step(t0 - 2)
                    act_step(t0 - 1)
            store0(0, J - 2)
            mm_step(STEPS - 2)
            act_step(STEPS - 2)
            mm_step(STEPS - 1)
            act_step(STEPS - 1)
            product(J - 2, J - 1)
            abs_max(B * (J - 2), B * (J - 1), out0[:, J * B + 7 : J * B + 8])
            product(J - 1, J)
            abs_max(B * (J - 1), J * B + 8, part[:, 0:1])
            store0(J - 2, J)
            spread = trp.tile([P, 2, 2, P], F32, name="bank", tag="bank")
            nc.tensor.transpose(spread[:, 0, 0, :], part[:, 0:1].to_broadcast([P, P]), ident[:])
            nc.vector.tensor_scalar(
                out=junk[:], in0=spread[:, 0, 0, :], scalar1=1.0 / 448.0, scalar2=None, op0=ALU.mult, op1=ALU.max, accum_out=scale[:, 0:1]
            )
            nc.vector.reciprocal(out=factor[:], in_=scale[:])
            nc.vector.tensor_scalar(
                out=out8[:, 0:V_CAST], in0=out0[:, 0:V_CAST], scalar1=factor[:, 0:1], scalar2=None, op0=ALU.mult, saturate=False
            )
            nc.scalar.activation(
                out=out8[:, V_CAST:], in_=out0[:, V_CAST : J * B], func=ACT.Identity, scale=factor[:, 0:1], bias=zero[:, 0:1], saturate=False
            )
            jv = V_CAST // B
            bytes8 = out8[:].bitcast(U8).rearrange("p (j b) -> p j b", b=B)
            nc.sync.dma_start(out=out1_v[:, 0:jv, :], in_=bytes8[:, 0:jv, :])
            nc.sync.dma_start(out=out1_v[:, jv:J, :], in_=bytes8[:, jv:J, :])
